import numpy as np
import ml_dtypes


def mxq(x, axis, fmt="e4m3"):
    dtype, down = {"e4m3": (ml_dtypes.float8_e4m3fn, 7), "e5m2": (ml_dtypes.float8_e5m2, 14)}[fmt]
    v = np.moveaxis(np.asarray(x, np.float32).astype(ml_dtypes.bfloat16).astype(np.float64), axis, -1)
    blocks = v.reshape(v.shape[:-1] + (-1, 32))
    amax = np.abs(blocks).max(-1, keepdims=True)
    byte = np.maximum(np.where(amax > 0, np.frexp(amax)[1] - 1 + 127, 0) - down, 1)
    scale = np.exp2(byte - 127.0)
    codes = (blocks / scale).astype(np.float32).astype(dtype).astype(np.float64)
    return np.moveaxis((codes * scale).reshape(v.shape), -1, axis)


WIDE = False


def mx_kscale(k):
    if not WIDE:
        return np.ones(k)
    levels = np.array([20, -20, 10, -10, 0])
    a = np.random.permutation(np.resize(levels, k // 512 * 4)).reshape(k // 512, 4)
    idx = np.arange(k)
    return np.exp2(a[idx // 512, idx % 128 // 32])


BF16 = ml_dtypes.bfloat16


def bf(x):
    return np.asarray(x, np.float32).astype(BF16)


def f64(x):
    return np.asarray(x).astype(np.float64)


B, P, L, K = 512, 8, 1024, 512
T = B * P
GAUSS_STD = 10.0


def setup_inputs():
    s = mx_kscale(T).reshape(B, P, 1)
    x = np.random.standard_normal((B, P, L)) * 0.5 * s
    weight = np.random.random(K) * L
    g = np.random.standard_normal((B, P, K)) * np.exp2(np.random.randint(-12, 1, (B, P, 1))) / s
    return {"x": bf(x.reshape(B, P * L)), "weight": bf(weight), "grad_out": bf(g.reshape(B, P * K))}


def reference(x, weight, grad_out):
    xt = f64(x).reshape(T, L)
    gt = f64(grad_out).reshape(T, K)
    G = mxq(xt, 0, "e4m3").T @ mxq(gt, 0, "e5m2")
    t = np.arange(1, L + 1, dtype=np.float64)
    d = t[:, None] - f64(weight)[None, :]
    D = np.exp(-(d ** 2) / (GAUSS_STD ** 2)) * (2.0 * d / (GAUSS_STD ** 2))
    return (G * D).sum(axis=0)

@@ -1,0 +1,169 @@
+from contextlib import ExitStack
+
+import concourse.mybir as mybir
+from concourse.masks import make_identity
+
+F32 = mybir.dt.float32
+BF16 = mybir.dt.bfloat16
+U32 = mybir.dt.uint32
+U8 = mybir.dt.uint8
+E4M3X4 = mybir.dt.float8_e4m3fn_x4
+E5M2X4 = mybir.dt.float8_e5m2_x4
+ACT = mybir.ActivationFunctionType
+ALU = mybir.AluOpType
+
+P = 128
+PACK = 4
+TOKENS = 4096
+L = 1024
+K = 512
+PASSES = TOKENS // (P * PACK)
+HALF = 512
+KT = K // P
+
+FLOPS = 2 * TOKENS * L * K
+
+SEQ = (
+    [("g", c, 0) for c in range(8)]
+    + [("x", c, h) for c in range(5) for h in range(2)]
+    + [("x", 5, 0), ("x", 6, 0), ("x", 7, 0), ("x", 5, 1), ("x", 6, 1), ("x", 7, 1)]
+)
+ON_SCALAR = [
+    ("g", 6, 0), ("g", 7, 0), ("x", 0, 0), ("x", 0, 1), ("x", 1, 1), ("x", 2, 1),
+    ("x", 3, 1), ("x", 4, 1), ("x", 6, 0), ("x", 5, 1), ("x", 6, 1), ("x", 7, 1),
+]
+AFTER = {
+    ("g", 1, 0): [("D", 0, 0)],
+    ("g", 3, 0): [("D", 1, 0)],
+    ("g", 5, 0): [("D", 2, 0)],
+    ("g", 7, 0): [("D", 3, 0)],
+    ("x", 5, 1): [("t", 0, 0), ("t", 1, 0)],
+    ("x", 6, 1): [("t", 2, 0), ("t", 3, 0)],
+    ("x", 7, 1): [("t", 0, 1), ("t", 1, 1), ("t", 2, 1), ("t", 3, 1)],
+}
+
+
+def tile_samplinglayer_kernel(tc, x, weight, grad_out, out):
+    nc = tc.nc
+    xv = x.rearrange("b (h j l) -> (b h) j l", h=2, j=PACK)
+    gv = grad_out.rearrange("b (h j k) -> (b h) j k", h=2, j=PACK)
+
+    with ExitStack() as ctx:
+        keep = ctx.enter_context(tc.tile_pool(name="keep", bufs=1))
+        grp_pool = ctx.enter_context(tc.tile_pool(name="grp", bufs=6))
+        xq_pool = ctx.enter_context(tc.tile_pool(name="xq", bufs=6))
+        work = ctx.enter_context(tc.tile_pool(name="work", bufs=2))
+        psum = ctx.enter_context(tc.psum_pool(name="psum", bufs=1))
+        ctx.enter_context(tc.manual_schedule())
+
+        wbf = keep.tile([P, KT], BF16, name="wbf")
+        with nc.allow_non_contiguous_dma(reason="512 sample positions, one to a partition"):
+            nc.scalar.dma_start(out=wbf[:], in_=weight.rearrange("(a p) -> p a", p=P))
+        raw = {}
+        for c in range(PASSES):
+            graw = keep.tile([P, PACK, K], BF16, name="graw%d" % c)
+            nc.sync.dma_start(out=graw[:], in_=gv[c * P : (c + 1) * P])
+            raw[("g", c)] = graw
+        for c in range(PASSES):
+            xraw = keep.tile([P, PACK, L], BF16, name="xraw%d" % c)
+            nc.sync.dma_start(out=xraw[:], in_=xv[c * P : (c + 1) * P])
+            raw[("x", c)] = xraw
+
+        tpos = keep.tile([P, L], F32, name="tpos")
+        nc.gpsimd.iota(
+            tpos[:, 0:P], pattern=[[1, P]], base=1, channel_multiplier=0,
+            allow_small_or_imprecise_dtypes=True,
+        )
+        ident = keep.tile([P, P], F32, name="ident")
+        make_identity(nc, ident[:])
+        sums = keep.tile([P, P], F32, name="sums")
+        nc.vector.memset(sums[:], 0.0)
+        width = P
+        while width < L:
+            nc.vector.tensor_scalar_add(tpos[:, width : 2 * width], tpos[:, 0:width], float(width))
+            width *= 2
+        negw = keep.tile([P, KT], F32, name="negw")
+        nc.vector.tensor_scalar_mul(negw[:], wbf[:], -1.0)
+
+        dmat = []
+        for kt in range(KT):
+            dk = keep.tile([P, L], F32, name="dmat%d" % kt)
+            nc.scalar.activation(out=dk[:], in_=tpos[:], func=ACT.Square, bias=negw[:, kt : kt + 1], scale=1.0)
+            nc.scalar.activation(out=dk[:], in_=dk[:], func=ACT.Exp, scale=-0.01)
+            dmat.append(dk)
+
+        banks = {}
+        for kt in range(KT):
+            for h in range(2):
+                banks[(kt, h)] = psum.tile([P, HALF], F32, name="G%d%d" % (kt, h))
+        acc = keep.tile([P, 2 * KT], F32, name="acc")
+        gq = {}
+        grouped = {}
+
+        def regroup(ch):
+            kind, c, h = ch
+            src = raw[(kind, c)][:, :, h * HALF : (h + 1) * HALF]
+            grp = grp_pool.tile([P, HALF, PACK], BF16, name="grp", align_bytes=64)
+            grouped[ch] = grp
+            dst_v = grp[:].rearrange("p (c i) t -> p c t i", i=4)
+            src_v = src.rearrange("p t (c i) -> p c t i", i=4)
+            if ch in ON_SCALAR:
+                nc.scalar.copy(out=dst_v, in_=src_v)
+            else:
+                nc.vector.tensor_copy(out=dst_v, in_=src_v)
+
+        def quantise(ch):
+            kind, c, h = ch
+            flat = grouped[ch][:].rearrange("p w t -> p (w t)")
+            if kind == "g":
+                codes = keep.tile([P, K], U32, name="gcodes%d" % c, align_bytes=64)
+                plane = keep.tile([P, K], U8, name="gplane%d" % c, align_bytes=64)
+                nc.vector.quantize_mx(out=codes[:].bitcast(E5M2X4), scales=plane[:], in_=flat)
+                gq[c] = (codes, plane)
+                return
+            codes = xq_pool.tile([P, HALF], U32, name="xcodes", align_bytes=64)
+            plane = xq_pool.tile([P, HALF], U8, name="xplane", align_bytes=64)
+            nc.vector.quantize_mx(out=codes[:].bitcast(E4M3X4), scales=plane[:], in_=flat)
+            gcodes, gplane = gq[c]
+            for kt in range(KT):
+                cols = slice(kt * P, (kt + 1) * P)
+                nc.tensor.matmul_mx(
+                    out=banks[(kt, h)][:],
+                    lhsT=gcodes[:, cols].bitcast(E5M2X4),
+                    lhsT_scale=gplane[:, cols],
+                    rhs=codes[:].bitcast(E4M3X4),
+                    rhs_scale=plane[:],
+                    start=(c == 0),
+                    stop=(c == PASSES - 1),
+                )
+
+        def extra(item):
+            kind, kt, h = item
+            if kind == "D":
+                nc.vector.scalar_tensor_tensor(
+                    out=dmat[kt][:], in0=tpos[:], scalar=negw[:, kt : kt + 1], in1=dmat[kt][:],
+                    op0=ALU.add, op1=ALU.mult,
+                )
+                return
+            junk = work.tile([P, HALF], F32, name="junk")
+            nc.vector.scalar_tensor_tensor(
+                out=junk[:], in0=banks[(kt, h)][:], scalar=1.0,
+                in1=dmat[kt][:, h * HALF : (h + 1) * HALF],
+                op0=ALU.mult, op1=ALU.mult,
+                accum_out=acc[:, h * KT + kt : h * KT + kt + 1],
+            )
+
+        for i in range(len(SEQ) + 1):
+            if i < len(SEQ):
+                regroup(SEQ[i])
+            if i >= 1:
+                quantise(SEQ[i - 1])
+                for item in AFTER.get(SEQ[i - 1], []):
+                    extra(item)
+
+        nc.vector.tensor_tensor(out=sums[:, 0:KT], in0=acc[:, 0:KT], in1=acc[:, KT : 2 * KT], op=ALU.add)
+        flipped = psum.tile([P, P], F32, name="flipped", tag="G00")
+        nc.tensor.transpose(flipped[:], sums[:], ident[:])
+        rows = keep.tile([P, P], F32, name="rows")
+        nc.scalar.activation(out=rows[:], in_=flipped[:], func=ACT.Copy, scale=0.02)
+        nc.sync.dma_start(out=out.rearrange("(a k) -> a k", a=KT), in_=rows[0:KT, :])

@@ -18,152 +18,156 @@ TOKENS = 4096
 L = 1024
 K = 512
 PASSES = TOKENS // (P * PACK)
-HALF = 512
-KT = K // P
+CHUNK = 512
+HALVES = L // CHUNK
+K_TILES = K // P
+
+G_AHEAD = 2
+HELD = 3
+VECTOR_ALONE = 6
+VECTOR_COLS = 192
 
 FLOPS = 2 * TOKENS * L * K
-
-SEQ = (
-    [("g", c, 0) for c in range(8)]
-    + [("x", c, h) for c in range(5) for h in range(2)]
-    + [("x", 5, 0), ("x", 6, 0), ("x", 7, 0), ("x", 5, 1), ("x", 6, 1), ("x", 7, 1)]
-)
-ON_SCALAR = [
-    ("g", 6, 0), ("g", 7, 0), ("x", 0, 0), ("x", 0, 1), ("x", 1, 1), ("x", 2, 1),
-    ("x", 3, 1), ("x", 4, 1), ("x", 6, 0), ("x", 5, 1), ("x", 6, 1), ("x", 7, 1),
-]
-AFTER = {
-    ("g", 1, 0): [("D", 0, 0)],
-    ("g", 3, 0): [("D", 1, 0)],
-    ("g", 5, 0): [("D", 2, 0)],
-    ("g", 7, 0): [("D", 3, 0)],
-    ("x", 5, 1): [("t", 0, 0), ("t", 1, 0)],
-    ("x", 6, 1): [("t", 2, 0), ("t", 3, 0)],
-    ("x", 7, 1): [("t", 0, 1), ("t", 1, 1), ("t", 2, 1), ("t", 3, 1)],
-}
 
 
 def tile_samplinglayer_kernel(tc, x, weight, grad_out, out):
     nc = tc.nc
-    xv = x.rearrange("b (h j l) -> (b h) j l", h=2, j=PACK)
-    gv = grad_out.rearrange("b (h j k) -> (b h) j k", h=2, j=PACK)
+    x_rows = x.rearrange("b (h j l) -> (b h) j l", h=2, j=PACK)
+    g_rows = grad_out.rearrange("b (h j k) -> (b h) j k", h=2, j=PACK)
+
+    loads = [("g", c) for c in range(G_AHEAD)]
+    chunks = [("g", c, 0) for c in range(G_AHEAD)]
+    for c in range(PASSES):
+        loads.append(("x", c))
+        chunks.append(("x", c, 0))
+        if c < PASSES - HELD:
+            chunks.append(("x", c, 1))
+        if c + G_AHEAD < PASSES:
+            loads.append(("g", c + G_AHEAD))
+            chunks.append(("g", c + G_AHEAD, 0))
+    chunks += [("x", c, 1) for c in range(PASSES - HELD, PASSES)]
+    first_held = len(chunks) - HELD
 
     with ExitStack() as ctx:
         keep = ctx.enter_context(tc.tile_pool(name="keep", bufs=1))
-        grp_pool = ctx.enter_context(tc.tile_pool(name="grp", bufs=6))
-        xq_pool = ctx.enter_context(tc.tile_pool(name="xq", bufs=6))
-        work = ctx.enter_context(tc.tile_pool(name="work", bufs=2))
+        grouped_pool = ctx.enter_context(tc.tile_pool(name="grouped", bufs=6))
+        x_pool = ctx.enter_context(tc.tile_pool(name="xq", bufs=4))
+        product_pool = ctx.enter_context(tc.tile_pool(name="product", bufs=2))
         psum = ctx.enter_context(tc.psum_pool(name="psum", bufs=1))
         ctx.enter_context(tc.manual_schedule())
 
-        wbf = keep.tile([P, KT], BF16, name="wbf")
+        w_bf16 = keep.tile([P, K_TILES], BF16, name="w_bf16")
         with nc.allow_non_contiguous_dma(reason="512 sample positions, one to a partition"):
-            nc.scalar.dma_start(out=wbf[:], in_=weight.rearrange("(a p) -> p a", p=P))
+            nc.scalar.dma_start(out=w_bf16[:], in_=weight.rearrange("(a p) -> p a", p=P))
         raw = {}
-        for c in range(PASSES):
-            graw = keep.tile([P, PACK, K], BF16, name="graw%d" % c)
-            nc.sync.dma_start(out=graw[:], in_=gv[c * P : (c + 1) * P])
-            raw[("g", c)] = graw
-        for c in range(PASSES):
-            xraw = keep.tile([P, PACK, L], BF16, name="xraw%d" % c)
-            nc.sync.dma_start(out=xraw[:], in_=xv[c * P : (c + 1) * P])
-            raw[("x", c)] = xraw
+        for kind, c in loads:
+            rows, cols = (g_rows, K) if kind == "g" else (x_rows, L)
+            raw[(kind, c)] = keep.tile([P, PACK, cols], BF16, name="raw_%s%d" % (kind, c))
+            nc.sync.dma_start(out=raw[(kind, c)][:], in_=rows[c * P : (c + 1) * P])
 
-        tpos = keep.tile([P, L], F32, name="tpos")
+        t_pos = keep.tile([P, L], F32, name="t_pos")
         nc.gpsimd.iota(
-            tpos[:, 0:P], pattern=[[1, P]], base=1, channel_multiplier=0,
+            t_pos[:, 0:P], pattern=[[1, P]], base=1, channel_multiplier=0,
             allow_small_or_imprecise_dtypes=True,
         )
-        ident = keep.tile([P, P], F32, name="ident")
-        make_identity(nc, ident[:])
+        identity = keep.tile([P, P], F32, name="identity")
+        make_identity(nc, identity[:])
         sums = keep.tile([P, P], F32, name="sums")
         nc.vector.memset(sums[:], 0.0)
-        width = P
-        while width < L:
-            nc.vector.tensor_scalar_add(tpos[:, width : 2 * width], tpos[:, 0:width], float(width))
-            width *= 2
-        negw = keep.tile([P, KT], F32, name="negw")
-        nc.vector.tensor_scalar_mul(negw[:], wbf[:], -1.0)
+        filled = P
+        while filled < L:
+            nc.vector.tensor_scalar_add(t_pos[:, filled : 2 * filled], t_pos[:, 0:filled], float(filled))
+            filled *= 2
+        neg_w = keep.tile([P, K_TILES], F32, name="neg_w")
+        nc.vector.tensor_scalar_mul(neg_w[:], w_bf16[:], -1.0)
 
-        dmat = []
-        for kt in range(KT):
-            dk = keep.tile([P, L], F32, name="dmat%d" % kt)
-            nc.scalar.activation(out=dk[:], in_=tpos[:], func=ACT.Square, bias=negw[:, kt : kt + 1], scale=1.0)
-            nc.scalar.activation(out=dk[:], in_=dk[:], func=ACT.Exp, scale=-0.01)
-            dmat.append(dk)
+        d_mat = [keep.tile([P, L], F32, name="d_mat%d" % kt) for kt in range(K_TILES)]
+        for kt in range(K_TILES):
+            nc.scalar.activation(
+                out=d_mat[kt][:], in_=t_pos[:], func=ACT.Square, bias=neg_w[:, kt : kt + 1], scale=1.0
+            )
+            nc.scalar.activation(out=d_mat[kt][:], in_=d_mat[kt][:], func=ACT.Exp, scale=-0.01)
 
         banks = {}
-        for kt in range(KT):
-            for h in range(2):
-                banks[(kt, h)] = psum.tile([P, HALF], F32, name="G%d%d" % (kt, h))
-        acc = keep.tile([P, 2 * KT], F32, name="acc")
-        gq = {}
+        for kt in range(K_TILES):
+            for h in range(HALVES):
+                banks[(kt, h)] = psum.tile([P, CHUNK], F32, name="bank%d%d" % (kt, h))
+        partial = keep.tile([P, HALVES * K_TILES], F32, name="partial")
+        g_codes = keep.tile([P, PASSES, K], U32, name="g_codes", align_bytes=64)
+        g_scales = keep.tile([P, PASSES, K], U8, name="g_scales", align_bytes=64)
         grouped = {}
 
-        def regroup(ch):
-            kind, c, h = ch
-            src = raw[(kind, c)][:, :, h * HALF : (h + 1) * HALF]
-            grp = grp_pool.tile([P, HALF, PACK], BF16, name="grp", align_bytes=64)
-            grouped[ch] = grp
-            dst_v = grp[:].rearrange("p (c i) t -> p c t i", i=4)
-            src_v = src.rearrange("p t (c i) -> p c t i", i=4)
-            if ch in ON_SCALAR:
-                nc.scalar.copy(out=dst_v, in_=src_v)
-            else:
-                nc.vector.tensor_copy(out=dst_v, in_=src_v)
+        def interleave(copy, dst, src):
+            copy(
+                out=dst.rearrange("p (c i) t -> p c t i", i=4),
+                in_=src.rearrange("p t (c i) -> p c t i", i=4),
+            )
 
-        def quantise(ch):
-            kind, c, h = ch
-            flat = grouped[ch][:].rearrange("p w t -> p (w t)")
+        def regroup(i):
+            kind, c, h = chunks[i]
+            src = raw[(kind, c)][:, :, h * CHUNK : (h + 1) * CHUNK]
+            grouped[i] = grouped_pool.tile([P, CHUNK, PACK], BF16, name="grouped", align_bytes=64)
+            cut = CHUNK if i < VECTOR_ALONE else VECTOR_COLS
+            interleave(nc.vector.tensor_copy, grouped[i][:, 0:cut, :], src[:, :, 0:cut])
+            if cut < CHUNK:
+                interleave(nc.scalar.copy, grouped[i][:, cut:CHUNK, :], src[:, :, cut:CHUNK])
+
+        def quantise_and_multiply(i):
+            kind, c, h = chunks[i]
+            flat = grouped[i][:].rearrange("p w t -> p (w t)")
             if kind == "g":
-                codes = keep.tile([P, K], U32, name="gcodes%d" % c, align_bytes=64)
-                plane = keep.tile([P, K], U8, name="gplane%d" % c, align_bytes=64)
-                nc.vector.quantize_mx(out=codes[:].bitcast(E5M2X4), scales=plane[:], in_=flat)
-                gq[c] = (codes, plane)
+                nc.vector.quantize_mx(
+                    out=g_codes[:, c, :].bitcast(E5M2X4), scales=g_scales[:, c, :], in_=flat
+                )
                 return
-            codes = xq_pool.tile([P, HALF], U32, name="xcodes", align_bytes=64)
-            plane = xq_pool.tile([P, HALF], U8, name="xplane", align_bytes=64)
-            nc.vector.quantize_mx(out=codes[:].bitcast(E4M3X4), scales=plane[:], in_=flat)
-            gcodes, gplane = gq[c]
-            for kt in range(KT):
-                cols = slice(kt * P, (kt + 1) * P)
+            x_codes = x_pool.tile([P, CHUNK], U32, name="x_codes", align_bytes=64)
+            x_scales = x_pool.tile([P, CHUNK], U8, name="x_scales", align_bytes=64)
+            nc.vector.quantize_mx(out=x_codes[:].bitcast(E4M3X4), scales=x_scales[:], in_=flat)
+            for kt in range(K_TILES):
+                k_cols = slice(kt * P, (kt + 1) * P)
                 nc.tensor.matmul_mx(
                     out=banks[(kt, h)][:],
-                    lhsT=gcodes[:, cols].bitcast(E5M2X4),
-                    lhsT_scale=gplane[:, cols],
-                    rhs=codes[:].bitcast(E4M3X4),
-                    rhs_scale=plane[:],
+                    lhsT=g_codes[:, c, k_cols].bitcast(E5M2X4),
+                    lhsT_scale=g_scales[:, c, k_cols],
+                    rhs=x_codes[:].bitcast(E4M3X4),
+                    rhs_scale=x_scales[:],
                     start=(c == 0),
                     stop=(c == PASSES - 1),
                 )
 
-        def extra(item):
-            kind, kt, h = item
-            if kind == "D":
-                nc.vector.scalar_tensor_tensor(
-                    out=dmat[kt][:], in0=tpos[:], scalar=negw[:, kt : kt + 1], in1=dmat[kt][:],
-                    op0=ALU.add, op1=ALU.mult,
-                )
-                return
-            junk = work.tile([P, HALF], F32, name="junk")
+        def finish_d(kt):
             nc.vector.scalar_tensor_tensor(
-                out=junk[:], in0=banks[(kt, h)][:], scalar=1.0,
-                in1=dmat[kt][:, h * HALF : (h + 1) * HALF],
-                op0=ALU.mult, op1=ALU.mult,
-                accum_out=acc[:, h * KT + kt : h * KT + kt + 1],
+                out=d_mat[kt][:], in0=t_pos[:], scalar=neg_w[:, kt : kt + 1], in1=d_mat[kt][:],
+                op0=ALU.add, op1=ALU.mult,
             )
 
-        for i in range(len(SEQ) + 1):
-            if i < len(SEQ):
-                regroup(SEQ[i])
-            if i >= 1:
-                quantise(SEQ[i - 1])
-                for item in AFTER.get(SEQ[i - 1], []):
-                    extra(item)
+        def weigh_and_sum(kt, h):
+            product = product_pool.tile([P, CHUNK], F32, name="product")
+            nc.vector.scalar_tensor_tensor(
+                out=product[:], in0=banks[(kt, h)][:], scalar=1.0,
+                in1=d_mat[kt][:, h * CHUNK : (h + 1) * CHUNK],
+                op0=ALU.mult, op1=ALU.mult,
+                accum_out=partial[:, h * K_TILES + kt : h * K_TILES + kt + 1],
+            )
 
-        nc.vector.tensor_tensor(out=sums[:, 0:KT], in0=acc[:, 0:KT], in1=acc[:, KT : 2 * KT], op=ALU.add)
-        flipped = psum.tile([P, P], F32, name="flipped", tag="G00")
-        nc.tensor.transpose(flipped[:], sums[:], ident[:])
-        rows = keep.tile([P, P], F32, name="rows")
-        nc.scalar.activation(out=rows[:], in_=flipped[:], func=ACT.Copy, scale=0.02)
-        nc.sync.dma_start(out=out.rearrange("(a k) -> a k", a=KT), in_=rows[0:KT, :])
+        regroup(0)
+        for i in range(len(chunks)):
+            if i + 1 < len(chunks):
+                regroup(i + 1)
+            quantise_and_multiply(i)
+            if i % 2 == 1 and i // 2 < K_TILES:
+                finish_d(i // 2)
+            if first_held <= i < first_held + 2:
+                weigh_and_sum(2 * (i - first_held), 0)
+                weigh_and_sum(2 * (i - first_held) + 1, 0)
+        for kt in range(K_TILES):
+            weigh_and_sum(kt, 1)
+
+        nc.vector.tensor_tensor(
+            out=sums[:, 0:K_TILES], in0=partial[:, 0:K_TILES], in1=partial[:, K_TILES : 2 * K_TILES], op=ALU.add
+        )
+        flipped = psum.tile([P, P], F32, name="flipped", tag="bank00")
+        nc.tensor.transpose(flipped[:], sums[:], identity[:])
+        out_rows = keep.tile([P, P], F32, name="out_rows")
+        nc.scalar.activation(out=out_rows[:], in_=flipped[:], func=ACT.Copy, scale=0.02)
+        nc.sync.dma_start(out=out.rearrange("(a k) -> a k", a=K_TILES), in_=out_rows[0:K_TILES, :])

@@ -18,14 +18,13 @@ TOKENS = 4096
 L = 1024
 K = 512
 PASSES = TOKENS // (P * PACK)
-CHUNK = 512
-HALVES = L // CHUNK
+BLOCK = 512
+UNIT = 2 * BLOCK
+HALVES = L // BLOCK
 K_TILES = K // P
 
-G_AHEAD = 2
-HELD = 3
-VECTOR_ALONE = 6
-VECTOR_COLS = 192
+VECTOR_ALONE = 3
+VECTOR_COLS = 384
 
 FLOPS = 2 * TOKENS * L * K
 
@@ -35,23 +34,21 @@ def tile_samplinglayer_kernel(tc, x, weight, grad_out, out):
     x_rows = x.rearrange("b (h j l) -> (b h) j l", h=2, j=PACK)
     g_rows = grad_out.rearrange("b (h j k) -> (b h) j k", h=2, j=PACK)
 
-    loads = [("g", c) for c in range(G_AHEAD)]
-    chunks = [("g", c, 0) for c in range(G_AHEAD)]
-    for c in range(PASSES):
-        loads.append(("x", c))
-        chunks.append(("x", c, 0))
-        if c < PASSES - HELD:
-            chunks.append(("x", c, 1))
-        if c + G_AHEAD < PASSES:
-            loads.append(("g", c + G_AHEAD))
-            chunks.append(("g", c + G_AHEAD, 0))
-    chunks += [("x", c, 1) for c in range(PASSES - HELD, PASSES)]
-    first_held = len(chunks) - HELD
+    units = []
+    for c in range(0, PASSES, 2):
+        units.append([("g", c, 0), ("g", c + 1, 0)])
+        if c + 2 < PASSES:
+            units.append([("x", c, 0), ("x", c, 1)])
+            units.append([("x", c + 1, 0), ("x", c + 1, 1)])
+        else:
+            units.append([("x", c, 0), ("x", c + 1, 0)])
+            units.append([("x", c, 1), ("x", c + 1, 1)])
+    last = len(units) - 1
 
     with ExitStack() as ctx:
         keep = ctx.enter_context(tc.tile_pool(name="keep", bufs=1))
-        grouped_pool = ctx.enter_context(tc.tile_pool(name="grouped", bufs=6))
-        x_pool = ctx.enter_context(tc.tile_pool(name="xq", bufs=4))
+        grouped_pool = ctx.enter_context(tc.tile_pool(name="grouped", bufs=4))
+        x_pool = ctx.enter_context(tc.tile_pool(name="xq", bufs=3))
         product_pool = ctx.enter_context(tc.tile_pool(name="product", bufs=2))
         psum = ctx.enter_context(tc.psum_pool(name="psum", bufs=1))
         ctx.enter_context(tc.manual_schedule())
@@ -59,11 +56,19 @@ def tile_samplinglayer_kernel(tc, x, weight, grad_out, out):
         w_bf16 = keep.tile([P, K_TILES], BF16, name="w_bf16")
         with nc.allow_non_contiguous_dma(reason="512 sample positions, one to a partition"):
             nc.scalar.dma_start(out=w_bf16[:], in_=weight.rearrange("(a p) -> p a", p=P))
-        raw = {}
-        for kind, c in loads:
-            rows, cols = (g_rows, K) if kind == "g" else (x_rows, L)
-            raw[(kind, c)] = keep.tile([P, PACK, cols], BF16, name="raw_%s%d" % (kind, c))
-            nc.sync.dma_start(out=raw[(kind, c)][:], in_=rows[c * P : (c + 1) * P])
+        raw = []
+        for u, blocks in enumerate(units):
+            raw.append(keep.tile([P, PACK, UNIT], BF16, name="raw%d" % u))
+            (kind, c, h), (kind_b, c_b, h_b) = blocks
+            if kind == "x" and c == c_b:
+                nc.sync.dma_start(out=raw[u][:], in_=x_rows[c * P : (c + 1) * P])
+                continue
+            for b, (kind, c, h) in enumerate(blocks):
+                rows = g_rows if kind == "g" else x_rows
+                nc.sync.dma_start(
+                    out=raw[u][:, :, b * BLOCK : (b + 1) * BLOCK],
+                    in_=rows[c * P : (c + 1) * P, :, h * BLOCK : (h + 1) * BLOCK],
+                )
 
         t_pos = keep.tile([P, L], F32, name="t_pos")
         nc.gpsimd.iota(
@@ -91,49 +96,54 @@ def tile_samplinglayer_kernel(tc, x, weight, grad_out, out):
         banks = {}
         for kt in range(K_TILES):
             for h in range(HALVES):
-                banks[(kt, h)] = psum.tile([P, CHUNK], F32, name="bank%d%d" % (kt, h))
+                banks[(kt, h)] = psum.tile([P, BLOCK], F32, name="bank%d%d" % (kt, h))
         partial = keep.tile([P, HALVES * K_TILES], F32, name="partial")
         g_codes = keep.tile([P, PASSES, K], U32, name="g_codes", align_bytes=64)
         g_scales = keep.tile([P, PASSES, K], U8, name="g_scales", align_bytes=64)
         grouped = {}
 
-        def interleave(copy, dst, src):
+        def interleave(copy, u, cols):
             copy(
-                out=dst.rearrange("p (c i) t -> p c t i", i=4),
-                in_=src.rearrange("p t (c i) -> p c t i", i=4),
+                out=grouped[u][:, cols, :].rearrange("p (c i) t -> p c t i", i=4),
+                in_=raw[u][:, :, cols].rearrange("p t (c i) -> p c t i", i=4),
             )
 
-        def regroup(i):
-            kind, c, h = chunks[i]
-            src = raw[(kind, c)][:, :, h * CHUNK : (h + 1) * CHUNK]
-            grouped[i] = grouped_pool.tile([P, CHUNK, PACK], BF16, name="grouped", align_bytes=64)
-            cut = CHUNK if i < VECTOR_ALONE else VECTOR_COLS
-            interleave(nc.vector.tensor_copy, grouped[i][:, 0:cut, :], src[:, :, 0:cut])
-            if cut < CHUNK:
-                interleave(nc.scalar.copy, grouped[i][:, cut:CHUNK, :], src[:, :, cut:CHUNK])
+        def regroup(u):
+            grouped[u] = grouped_pool.tile([P, UNIT, PACK], BF16, name="grouped", align_bytes=64)
+            if u < VECTOR_ALONE:
+                interleave(nc.vector.tensor_copy, u, slice(0, BLOCK))
+                interleave(nc.vector.tensor_copy, u, slice(BLOCK, UNIT))
+            else:
+                interleave(nc.vector.tensor_copy, u, slice(0, VECTOR_COLS))
+                interleave(nc.scalar.copy, u, slice(VECTOR_COLS, UNIT))
 
-        def quantise_and_multiply(i):
-            kind, c, h = chunks[i]
-            flat = grouped[i][:].rearrange("p w t -> p (w t)")
-            if kind == "g":
+        def quantise_and_multiply(u):
+            blocks = units[u]
+            flat = grouped[u][:].rearrange("p w t -> p (w t)")
+            if blocks[0][0] == "g":
+                c = blocks[0][1]
                 nc.vector.quantize_mx(
-                    out=g_codes[:, c, :].bitcast(E5M2X4), scales=g_scales[:, c, :], in_=flat
+                    out=g_codes[:, c : c + 2, :].rearrange("p c k -> p (c k)").bitcast(E5M2X4),
+                    scales=g_scales[:, c : c + 2, :].rearrange("p c k -> p (c k)"),
+                    in_=flat,
                 )
                 return
-            x_codes = x_pool.tile([P, CHUNK], U32, name="x_codes", align_bytes=64)
-            x_scales = x_pool.tile([P, CHUNK], U8, name="x_scales", align_bytes=64)
+            x_codes = x_pool.tile([P, UNIT], U32, name="x_codes", align_bytes=64)
+            x_scales = x_pool.tile([P, UNIT], U8, name="x_scales", align_bytes=64)
             nc.vector.quantize_mx(out=x_codes[:].bitcast(E4M3X4), scales=x_scales[:], in_=flat)
             for kt in range(K_TILES):
                 k_cols = slice(kt * P, (kt + 1) * P)
-                nc.tensor.matmul_mx(
-                    out=banks[(kt, h)][:],
-                    lhsT=g_codes[:, c, k_cols].bitcast(E5M2X4),
-                    lhsT_scale=g_scales[:, c, k_cols],
-                    rhs=x_codes[:].bitcast(E4M3X4),
-                    rhs_scale=x_scales[:],
-                    start=(c == 0),
-                    stop=(c == PASSES - 1),
-                )
+                for b, (kind, c, h) in enumerate(blocks):
+                    l_cols = slice(b * BLOCK, (b + 1) * BLOCK)
+                    nc.tensor.matmul_mx(
+                        out=banks[(kt, h)][:],
+                        lhsT=g_codes[:, c, k_cols].bitcast(E5M2X4),
+                        lhsT_scale=g_scales[:, c, k_cols],
+                        rhs=x_codes[:, l_cols].bitcast(E4M3X4),
+                        rhs_scale=x_scales[:, l_cols],
+                        start=(c == 0),
+                        stop=(c == PASSES - 1),
+                    )
 
         def finish_d(kt):
             nc.vector.scalar_tensor_tensor(
@@ -142,26 +152,26 @@ def tile_samplinglayer_kernel(tc, x, weight, grad_out, out):
             )
 
         def weigh_and_sum(kt, h):
-            product = product_pool.tile([P, CHUNK], F32, name="product")
+            product = product_pool.tile([P, BLOCK], F32, name="product")
             nc.vector.scalar_tensor_tensor(
                 out=product[:], in0=banks[(kt, h)][:], scalar=1.0,
-                in1=d_mat[kt][:, h * CHUNK : (h + 1) * CHUNK],
+                in1=d_mat[kt][:, h * BLOCK : (h + 1) * BLOCK],
                 op0=ALU.mult, op1=ALU.mult,
                 accum_out=partial[:, h * K_TILES + kt : h * K_TILES + kt + 1],
             )
 
         regroup(0)
-        for i in range(len(chunks)):
-            if i + 1 < len(chunks):
-                regroup(i + 1)
-            quantise_and_multiply(i)
-            if i % 2 == 1 and i // 2 < K_TILES:
-                finish_d(i // 2)
-            if first_held <= i < first_held + 2:
-                weigh_and_sum(2 * (i - first_held), 0)
-                weigh_and_sum(2 * (i - first_held) + 1, 0)
-        for kt in range(K_TILES):
-            weigh_and_sum(kt, 1)
+        for u in range(len(units)):
+            if u < last:
+                regroup(u + 1)
+            quantise_and_multiply(u)
+            if u < K_TILES - 1:
+                finish_d(u)
+            if u == last - 1:
+                finish_d(K_TILES - 1)
+            if u >= last - 1:
+                for kt in range(K_TILES):
+                    weigh_and_sum(kt, u - (last - 1))
 
         nc.vector.tensor_tensor(
             out=sums[:, 0:K_TILES], in0=partial[:, 0:K_TILES], in1=partial[:, K_TILES : 2 * K_TILES], op=ALU.add

@@ -18,13 +18,10 @@ TOKENS = 4096
 L = 1024
 K = 512
 PASSES = TOKENS // (P * PACK)
-BLOCK = 512
-UNIT = 2 * BLOCK
-HALVES = L // BLOCK
+CHUNK = 512
+HALVES = L // CHUNK
 K_TILES = K // P
-
-VECTOR_ALONE = 3
-VECTOR_COLS = 384
+SHARED_COLS = 256
 
 FLOPS = 2 * TOKENS * L * K
 
@@ -34,41 +31,34 @@ def tile_samplinglayer_kernel(tc, x, weight, grad_out, out):
     x_rows = x.rearrange("b (h j l) -> (b h) j l", h=2, j=PACK)
     g_rows = grad_out.rearrange("b (h j k) -> (b h) j k", h=2, j=PACK)
 
-    units = []
-    for c in range(0, PASSES, 2):
-        units.append([("g", c, 0), ("g", c + 1, 0)])
-        if c + 2 < PASSES:
-            units.append([("x", c, 0), ("x", c, 1)])
-            units.append([("x", c + 1, 0), ("x", c + 1, 1)])
-        else:
-            units.append([("x", c, 0), ("x", c + 1, 0)])
-            units.append([("x", c, 1), ("x", c + 1, 1)])
-    last = len(units) - 1
+    scalar_chunks = []
+    for c in range(PASSES // 2):
+        scalar_chunks += [("g", c + PASSES // 2, 0), ("x", c, 1)]
+    scalar_chunks += [("x", c, 1) for c in range(PASSES // 2, PASSES)]
+    chunks = [("g", c, 0) for c in range(PASSES // 2)]
+    for c in range(PASSES):
+        chunks += [("x", c, 0), scalar_chunks[c]]
+    chunks += scalar_chunks[PASSES:]
+    last = len(chunks) - 1
+    first_half_closed = chunks.index(("x", PASSES - 1, 0)) + 2
 
     with ExitStack() as ctx:
         keep = ctx.enter_context(tc.tile_pool(name="keep", bufs=1))
-        grouped_pool = ctx.enter_context(tc.tile_pool(name="grouped", bufs=4))
-        x_pool = ctx.enter_context(tc.tile_pool(name="xq", bufs=3))
+        grouped_pool = ctx.enter_context(tc.tile_pool(name="grouped", bufs=6))
+        x_pool = ctx.enter_context(tc.tile_pool(name="xq", bufs=4))
         product_pool = ctx.enter_context(tc.tile_pool(name="product", bufs=2))
         psum = ctx.enter_context(tc.psum_pool(name="psum", bufs=1))
         ctx.enter_context(tc.manual_schedule())
 
-        w_bf16 = keep.tile([P, K_TILES], BF16, name="w_bf16")
+        w_col = keep.tile([P, K_TILES], BF16, name="w_col")
         with nc.allow_non_contiguous_dma(reason="512 sample positions, one to a partition"):
-            nc.scalar.dma_start(out=w_bf16[:], in_=weight.rearrange("(a p) -> p a", p=P))
-        raw = []
-        for u, blocks in enumerate(units):
-            raw.append(keep.tile([P, PACK, UNIT], BF16, name="raw%d" % u))
-            (kind, c, h), (kind_b, c_b, h_b) = blocks
-            if kind == "x" and c == c_b:
-                nc.sync.dma_start(out=raw[u][:], in_=x_rows[c * P : (c + 1) * P])
-                continue
-            for b, (kind, c, h) in enumerate(blocks):
-                rows = g_rows if kind == "g" else x_rows
-                nc.sync.dma_start(
-                    out=raw[u][:, :, b * BLOCK : (b + 1) * BLOCK],
-                    in_=rows[c * P : (c + 1) * P, :, h * BLOCK : (h + 1) * BLOCK],
-                )
+            nc.scalar.dma_start(out=w_col[:], in_=weight.rearrange("(a p) -> p a", p=P))
+        raw = {}
+        for kind, c, h in chunks:
+            if (kind, c) not in raw:
+                rows, cols = (g_rows, K) if kind == "g" else (x_rows, L)
+                raw[(kind, c)] = keep.tile([P, PACK, cols], BF16, name="raw_%s%d" % (kind, c))
+                nc.sync.dma_start(out=raw[(kind, c)][:], in_=rows[c * P : (c + 1) * P])
 
         t_pos = keep.tile([P, L], F32, name="t_pos")
         nc.gpsimd.iota(
@@ -83,95 +73,93 @@ def tile_samplinglayer_kernel(tc, x, weight, grad_out, out):
         while filled < L:
             nc.vector.tensor_scalar_add(t_pos[:, filled : 2 * filled], t_pos[:, 0:filled], float(filled))
             filled *= 2
-        neg_w = keep.tile([P, K_TILES], F32, name="neg_w")
-        nc.vector.tensor_scalar_mul(neg_w[:], w_bf16[:], -1.0)
 
-        d_mat = [keep.tile([P, L], F32, name="d_mat%d" % kt) for kt in range(K_TILES)]
+        d_mat = keep.tile([P, K_TILES, L], F32, name="d_mat")
         for kt in range(K_TILES):
             nc.scalar.activation(
-                out=d_mat[kt][:], in_=t_pos[:], func=ACT.Square, bias=neg_w[:, kt : kt + 1], scale=1.0
+                out=d_mat[:, kt, :], in_=t_pos[:], func=ACT.Square, bias=w_col[:, kt : kt + 1], scale=-1.0
             )
-            nc.scalar.activation(out=d_mat[kt][:], in_=d_mat[kt][:], func=ACT.Exp, scale=-0.01)
+        nc.scalar.activation(out=d_mat[:], in_=d_mat[:], func=ACT.Exp, scale=-0.01)
 
         banks = {}
         for kt in range(K_TILES):
             for h in range(HALVES):
-                banks[(kt, h)] = psum.tile([P, BLOCK], F32, name="bank%d%d" % (kt, h))
+                banks[(kt, h)] = psum.tile([P, CHUNK], F32, name="bank%d%d" % (kt, h))
         partial = keep.tile([P, HALVES * K_TILES], F32, name="partial")
         g_codes = keep.tile([P, PASSES, K], U32, name="g_codes", align_bytes=64)
         g_scales = keep.tile([P, PASSES, K], U8, name="g_scales", align_bytes=64)
         grouped = {}
 
-        def interleave(copy, u, cols):
+        def interleave(copy, dst, src):
             copy(
-                out=grouped[u][:, cols, :].rearrange("p (c i) t -> p c t i", i=4),
-                in_=raw[u][:, :, cols].rearrange("p t (c i) -> p c t i", i=4),
+                out=dst.rearrange("p (c i) t -> p c t i", i=4),
+                in_=src.rearrange("p t (c i) -> p c t i", i=4),
             )
 
-        def regroup(u):
-            grouped[u] = grouped_pool.tile([P, UNIT, PACK], BF16, name="grouped", align_bytes=64)
-            if u < VECTOR_ALONE:
-                interleave(nc.vector.tensor_copy, u, slice(0, BLOCK))
-                interleave(nc.vector.tensor_copy, u, slice(BLOCK, UNIT))
+        def regroup(i):
+            kind, c, h = chunks[i]
+            src = raw[(kind, c)][:, :, h * CHUNK : (h + 1) * CHUNK]
+            grouped[i] = grouped_pool.tile([P, CHUNK, PACK], BF16, name="grouped", align_bytes=64)
+            if i == last:
+                cut = SHARED_COLS
+            elif chunks[i] in scalar_chunks:
+                cut = 0
             else:
-                interleave(nc.vector.tensor_copy, u, slice(0, VECTOR_COLS))
-                interleave(nc.scalar.copy, u, slice(VECTOR_COLS, UNIT))
+                cut = CHUNK
+            if cut > 0:
+                interleave(nc.vector.tensor_copy, grouped[i][:, 0:cut, :], src[:, :, 0:cut])
+            if cut < CHUNK:
+                interleave(nc.scalar.copy, grouped[i][:, cut:CHUNK, :], src[:, :, cut:CHUNK])
 
-        def quantise_and_multiply(u):
-            blocks = units[u]
-            flat = grouped[u][:].rearrange("p w t -> p (w t)")
-            if blocks[0][0] == "g":
-                c = blocks[0][1]
+        def quantise_and_multiply(i):
+            kind, c, h = chunks[i]
+            flat = grouped[i][:].rearrange("p w t -> p (w t)")
+            if kind == "g":
                 nc.vector.quantize_mx(
-                    out=g_codes[:, c : c + 2, :].rearrange("p c k -> p (c k)").bitcast(E5M2X4),
-                    scales=g_scales[:, c : c + 2, :].rearrange("p c k -> p (c k)"),
-                    in_=flat,
+                    out=g_codes[:, c, :].bitcast(E5M2X4), scales=g_scales[:, c, :], in_=flat
                 )
                 return
-            x_codes = x_pool.tile([P, UNIT], U32, name="x_codes", align_bytes=64)
-            x_scales = x_pool.tile([P, UNIT], U8, name="x_scales", align_bytes=64)
+            x_codes = x_pool.tile([P, CHUNK], U32, name="x_codes", align_bytes=64)
+            x_scales = x_pool.tile([P, CHUNK], U8, name="x_scales", align_bytes=64)
             nc.vector.quantize_mx(out=x_codes[:].bitcast(E4M3X4), scales=x_scales[:], in_=flat)
             for kt in range(K_TILES):
                 k_cols = slice(kt * P, (kt + 1) * P)
-                for b, (kind, c, h) in enumerate(blocks):
-                    l_cols = slice(b * BLOCK, (b + 1) * BLOCK)
-                    nc.tensor.matmul_mx(
-                        out=banks[(kt, h)][:],
-                        lhsT=g_codes[:, c, k_cols].bitcast(E5M2X4),
-                        lhsT_scale=g_scales[:, c, k_cols],
-                        rhs=x_codes[:, l_cols].bitcast(E4M3X4),
-                        rhs_scale=x_scales[:, l_cols],
-                        start=(c == 0),
-                        stop=(c == PASSES - 1),
-                    )
+                nc.tensor.matmul_mx(
+                    out=banks[(kt, h)][:],
+                    lhsT=g_codes[:, c, k_cols].bitcast(E5M2X4),
+                    lhsT_scale=g_scales[:, c, k_cols],
+                    rhs=x_codes[:].bitcast(E4M3X4),
+                    rhs_scale=x_scales[:],
+                    start=(c == 0),
+                    stop=(c == PASSES - 1),
+                )
 
         def finish_d(kt):
             nc.vector.scalar_tensor_tensor(
-                out=d_mat[kt][:], in0=t_pos[:], scalar=neg_w[:, kt : kt + 1], in1=d_mat[kt][:],
-                op0=ALU.add, op1=ALU.mult,
+                out=d_mat[:, kt, :], in0=t_pos[:], scalar=w_col[:, kt : kt + 1], in1=d_mat[:, kt, :],
+                op0=ALU.subtract, op1=ALU.mult,
             )
 
         def weigh_and_sum(kt, h):
-            product = product_pool.tile([P, BLOCK], F32, name="product")
+            product = product_pool.tile([P, CHUNK], F32, name="product")
             nc.vector.scalar_tensor_tensor(
                 out=product[:], in0=banks[(kt, h)][:], scalar=1.0,
-                in1=d_mat[kt][:, h * BLOCK : (h + 1) * BLOCK],
+                in1=d_mat[:, kt, h * CHUNK : (h + 1) * CHUNK],
                 op0=ALU.mult, op1=ALU.mult,
                 accum_out=partial[:, h * K_TILES + kt : h * K_TILES + kt + 1],
             )
 
         regroup(0)
-        for u in range(len(units)):
-            if u < last:
-                regroup(u + 1)
-            quantise_and_multiply(u)
-            if u < K_TILES - 1:
-                finish_d(u)
-            if u == last - 1:
-                finish_d(K_TILES - 1)
-            if u >= last - 1:
-                for kt in range(K_TILES):
-                    weigh_and_sum(kt, u - (last - 1))
+        for i in range(len(chunks)):
+            if i < last:
+                regroup(i + 1)
+            quantise_and_multiply(i)
+            if PASSES // 2 <= i < PASSES // 2 + K_TILES:
+                finish_d(i - PASSES // 2)
+            if first_half_closed <= i < first_half_closed + K_TILES:
+                weigh_and_sum(i - first_half_closed, 0)
+        for kt in range(K_TILES):
+            weigh_and_sum(kt, 1)
 
         nc.vector.tensor_tensor(
             out=sums[:, 0:K_TILES], in0=partial[:, 0:K_TILES], in1=partial[:, K_TILES : 2 * K_TILES], op=ALU.add

@@ -50,6 +50,9 @@ def tile_samplinglayer_kernel(tc, x, weight, grad_out, out):
         psum = ctx.enter_context(tc.psum_pool(name="psum", bufs=1))
         ctx.enter_context(tc.manual_schedule())
 
+        warm = keep.tile([P, 1], F32, name="warm")
+        nc.vector.memset(warm[:], 0.0)
+        nc.scalar.activation(out=warm[:], in_=warm[:], func=ACT.Exp)
         w_col = keep.tile([P, K_TILES], BF16, name="w_col")
         with nc.allow_non_contiguous_dma(reason="512 sample positions, one to a partition"):
             nc.scalar.dma_start(out=w_col[:], in_=weight.rearrange("(a p) -> p a", p=P))

@@ -50,12 +50,12 @@ def tile_samplinglayer_kernel(tc, x, weight, grad_out, out):
         psum = ctx.enter_context(tc.psum_pool(name="psum", bufs=1))
         ctx.enter_context(tc.manual_schedule())
 
-        warm = keep.tile([P, 1], F32, name="warm")
-        nc.vector.memset(warm[:], 0.0)
-        nc.scalar.activation(out=warm[:], in_=warm[:], func=ACT.Exp)
         w_col = keep.tile([P, K_TILES], BF16, name="w_col")
         with nc.allow_non_contiguous_dma(reason="512 sample positions, one to a partition"):
             nc.scalar.dma_start(out=w_col[:], in_=weight.rearrange("(a p) -> p a", p=P))
+        warm = keep.tile([P, 1], F32, name="warm")
+        nc.vector.memset(warm[:], 0.0)
+        nc.scalar.activation(out=warm[:], in_=warm[:], func=ACT.Exp)
         raw = {}
         for kind, c, h in chunks:
             if (kind, c) not in raw:

@@ -44,7 +44,7 @@ def tile_samplinglayer_kernel(tc, x, weight, grad_out, out):
 
     with ExitStack() as ctx:
         keep = ctx.enter_context(tc.tile_pool(name="keep", bufs=1))
-        grouped_pool = ctx.enter_context(tc.tile_pool(name="grouped", bufs=6))
+        grouped_pool = ctx.enter_context(tc.tile_pool(name="grouped", bufs=8))
         x_pool = ctx.enter_context(tc.tile_pool(name="xq", bufs=4))
         product_pool = ctx.enter_context(tc.tile_pool(name="product", bufs=2))
         psum = ctx.enter_context(tc.psum_pool(name="psum", bufs=1))
@@ -56,12 +56,16 @@ def tile_samplinglayer_kernel(tc, x, weight, grad_out, out):
         warm = keep.tile([P, 1], F32, name="warm")
         nc.vector.memset(warm[:], 0.0)
         nc.scalar.activation(out=warm[:], in_=warm[:], func=ACT.Exp)
+        loads = [("g", c) for c in range(PASSES // 2)]
+        for c in range(PASSES):
+            loads.append(("x", c))
+            if c < PASSES // 2:
+                loads.append(("g", c + PASSES // 2))
         raw = {}
-        for kind, c, h in chunks:
-            if (kind, c) not in raw:
-                rows, cols = (g_rows, K) if kind == "g" else (x_rows, L)
-                raw[(kind, c)] = keep.tile([P, PACK, cols], BF16, name="raw_%s%d" % (kind, c))
-                nc.sync.dma_start(out=raw[(kind, c)][:], in_=rows[c * P : (c + 1) * P])
+        for kind, c in loads:
+            rows, cols = (g_rows, K) if kind == "g" else (x_rows, L)
+            raw[(kind, c)] = keep.tile([P, PACK, cols], BF16, name="raw_%s%d" % (kind, c))
+            nc.sync.dma_start(out=raw[(kind, c)][:], in_=rows[c * P : (c + 1) * P])
 
         t_pos = keep.tile([P, L], F32, name="t_pos")
         nc.gpsimd.iota(

@@ -21,7 +21,7 @@ PASSES = TOKENS // (P * PACK)
 CHUNK = 512
 HALVES = L // CHUNK
 K_TILES = K // P
-SHARED_COLS = 256
+SHARED_COLS = 384
 
 FLOPS = 2 * TOKENS * L * K
 
@@ -40,11 +40,11 @@ def tile_samplinglayer_kernel(tc, x, weight, grad_out, out):
         chunks += [("x", c, 0), scalar_chunks[c]]
     chunks += scalar_chunks[PASSES:]
     last = len(chunks) - 1
-    first_half_closed = chunks.index(("x", PASSES - 1, 0)) + 2
 
     with ExitStack() as ctx:
         keep = ctx.enter_context(tc.tile_pool(name="keep", bufs=1))
         grouped_pool = ctx.enter_context(tc.tile_pool(name="grouped", bufs=8))
+        late_pool = ctx.enter_context(tc.tile_pool(name="late", bufs=1))
         x_pool = ctx.enter_context(tc.tile_pool(name="xq", bufs=4))
         product_pool = ctx.enter_context(tc.tile_pool(name="product", bufs=2))
         psum = ctx.enter_context(tc.psum_pool(name="psum", bufs=1))
@@ -56,11 +56,11 @@ def tile_samplinglayer_kernel(tc, x, weight, grad_out, out):
         warm = keep.tile([P, 1], F32, name="warm")
         nc.vector.memset(warm[:], 0.0)
         nc.scalar.activation(out=warm[:], in_=warm[:], func=ACT.Exp)
-        loads = [("g", c) for c in range(PASSES // 2)]
+        loads = [("g", 0), ("g", 1), ("g", 2), ("g", 4), ("g", 3)]
         for c in range(PASSES):
             loads.append(("x", c))
-            if c < PASSES // 2:
-                loads.append(("g", c + PASSES // 2))
+            if c < PASSES // 2 - 1:
+                loads.append(("g", c + PASSES // 2 + 1))
         raw = {}
         for kind, c in loads:
             rows, cols = (g_rows, K) if kind == "g" else (x_rows, L)
@@ -81,12 +81,24 @@ def tile_samplinglayer_kernel(tc, x, weight, grad_out, out):
             nc.vector.tensor_scalar_add(t_pos[:, filled : 2 * filled], t_pos[:, 0:filled], float(filled))
             filled *= 2
 
-        d_mat = keep.tile([P, K_TILES, L], F32, name="d_mat")
+        distance = keep.tile([P, K_TILES, CHUNK], F32, name="distance")
         for kt in range(K_TILES):
-            nc.scalar.activation(
-                out=d_mat[:, kt, :], in_=t_pos[:], func=ACT.Square, bias=w_col[:, kt : kt + 1], scale=-1.0
+            nc.vector.tensor_scalar(
+                out=distance[:, kt, :], in0=t_pos[:, CHUNK:L], scalar1=w_col[:, kt : kt + 1], scalar2=None,
+                op0=ALU.subtract,
             )
-        nc.scalar.activation(out=d_mat[:], in_=d_mat[:], func=ACT.Exp, scale=-0.01)
+
+        d_mat = keep.tile([P, K_TILES, L], F32, name="d_mat")
+
+        def square(kt, h):
+            cols = slice(h * CHUNK, (h + 1) * CHUNK)
+            nc.scalar.activation(
+                out=d_mat[:, kt, cols], in_=t_pos[:, cols], func=ACT.Square, bias=w_col[:, kt : kt + 1], scale=-1.0
+            )
+
+        for kt in range(K_TILES):
+            square(kt, 0)
+        nc.scalar.activation(out=d_mat[:, :, 0:CHUNK], in_=d_mat[:, :, 0:CHUNK], func=ACT.Exp, scale=-0.01)
 
         banks = {}
         for kt in range(K_TILES):
@@ -106,7 +118,10 @@ def tile_samplinglayer_kernel(tc, x, weight, grad_out, out):
         def regroup(i):
             kind, c, h = chunks[i]
             src = raw[(kind, c)][:, :, h * CHUNK : (h + 1) * CHUNK]
-            grouped[i] = grouped_pool.tile([P, CHUNK, PACK], BF16, name="grouped", align_bytes=64)
+            if i >= last - 1:
+                grouped[i] = late_pool.tile([P, CHUNK, PACK], BF16, name="late%d" % (last - i), align_bytes=64)
+            else:
+                grouped[i] = grouped_pool.tile([P, CHUNK, PACK], BF16, name="grouped", align_bytes=64)
             if i == last:
                 cut = SHARED_COLS
             elif chunks[i] in scalar_chunks:
@@ -143,15 +158,17 @@ def tile_samplinglayer_kernel(tc, x, weight, grad_out, out):
 
         def finish_d(kt):
             nc.vector.scalar_tensor_tensor(
-                out=d_mat[:, kt, :], in0=t_pos[:], scalar=w_col[:, kt : kt + 1], in1=d_mat[:, kt, :],
-                op0=ALU.subtract, op1=ALU.mult,
+                out=d_mat[:, kt, 0:CHUNK], in0=t_pos[:, 0:CHUNK], scalar=w_col[:, kt : kt + 1],
+                in1=d_mat[:, kt, 0:CHUNK], op0=ALU.subtract, op1=ALU.mult,
             )
+
+        second = {}
 
         def weigh_and_sum(kt, h):
             product = product_pool.tile([P, CHUNK], F32, name="product")
             nc.vector.scalar_tensor_tensor(
                 out=product[:], in0=banks[(kt, h)][:], scalar=1.0,
-                in1=d_mat[:, kt, h * CHUNK : (h + 1) * CHUNK],
+                in1=d_mat[:, kt, 0:CHUNK] if h == 0 else second[kt],
                 op0=ALU.mult, op1=ALU.mult,
                 accum_out=partial[:, h * K_TILES + kt : h * K_TILES + kt + 1],
             )
@@ -163,8 +180,17 @@ def tile_samplinglayer_kernel(tc, x, weight, grad_out, out):
             quantise_and_multiply(i)
             if PASSES // 2 <= i < PASSES // 2 + K_TILES:
                 finish_d(i - PASSES // 2)
-            if first_half_closed <= i < first_half_closed + K_TILES:
-                weigh_and_sum(i - first_half_closed, 0)
+        for kt in range(K_TILES):
+            square(kt, 1)
+            nc.scalar.activation(out=d_mat[:, kt, CHUNK:L], in_=d_mat[:, kt, CHUNK:L], func=ACT.Exp, scale=-0.01)
+        for pair in range(K_TILES // 2):
+            late = late_pool.tile([P, 2, CHUNK], F32, name="late%d" % pair, align_bytes=64)
+            for j in range(2):
+                kt = 2 * pair + j
+                second[kt] = late[:, j, :]
+                nc.gpsimd.tensor_tensor(out=second[kt], in0=distance[:, kt, :], in1=d_mat[:, kt, CHUNK:L], op=ALU.mult)
+        for kt in range(K_TILES):
+            weigh_and_sum(kt, 0)
         for kt in range(K_TILES):
             weigh_and_sum(kt, 1)
 

@@ -21,7 +21,7 @@ PASSES = TOKENS // (P * PACK)
 CHUNK = 512
 HALVES = L // CHUNK
 K_TILES = K // P
-SHARED_COLS = 384
+SHARED_COLS = 256
 
 FLOPS = 2 * TOKENS * L * K
 
@@ -111,13 +111,15 @@ def tile_samplinglayer_kernel(tc, x, weight, grad_out, out):
 
         def interleave(copy, dst, src):
             copy(
-                out=dst.rearrange("p (c i) t -> p c t i", i=4),
-                in_=src.rearrange("p t (c i) -> p c t i", i=4),
+                out=dst.rearrange("p (c i) t -> p c t i", i=8),
+                in_=src.rearrange("p t (c i) -> p c t i", i=8),
             )
 
         def regroup(i):
             kind, c, h = chunks[i]
             src = raw[(kind, c)][:, :, h * CHUNK : (h + 1) * CHUNK]
+            if chunks[i] == ("x", 0, 1):
+                square(0, 1)
             if i >= last - 1:
                 grouped[i] = late_pool.tile([P, CHUNK, PACK], BF16, name="late%d" % (last - i), align_bytes=64)
             else:
@@ -181,7 +183,8 @@ def tile_samplinglayer_kernel(tc, x, weight, grad_out, out):
             if PASSES // 2 <= i < PASSES // 2 + K_TILES:
                 finish_d(i - PASSES // 2)
         for kt in range(K_TILES):
-            square(kt, 1)
+            if kt > 0:
+                square(kt, 1)
             nc.scalar.activation(out=d_mat[:, kt, CHUNK:L], in_=d_mat[:, kt, CHUNK:L], func=ACT.Exp, scale=-0.01)
         for pair in range(K_TILES // 2):
             late = late_pool.tile([P, 2, CHUNK], F32, name="late%d" % pair, align_bytes=64)

@@ -22,6 +22,7 @@ CHUNK = 512
 HALVES = L // CHUNK
 K_TILES = K // P
 SHARED_COLS = 256
+GPSIMD_COLS = 384
 
 FLOPS = 2 * TOKENS * L * K
 
@@ -43,9 +44,10 @@ def tile_samplinglayer_kernel(tc, x, weight, grad_out, out):
 
     with ExitStack() as ctx:
         keep = ctx.enter_context(tc.tile_pool(name="keep", bufs=1))
-        grouped_pool = ctx.enter_context(tc.tile_pool(name="grouped", bufs=8))
+        grouped_pool = ctx.enter_context(tc.tile_pool(name="grouped", bufs=12))
         late_pool = ctx.enter_context(tc.tile_pool(name="late", bufs=1))
-        x_pool = ctx.enter_context(tc.tile_pool(name="xq", bufs=4))
+        early_pool = ctx.enter_context(tc.tile_pool(name="early", bufs=1))
+        x_pool = ctx.enter_context(tc.tile_pool(name="xq", bufs=6))
         product_pool = ctx.enter_context(tc.tile_pool(name="product", bufs=2))
         psum = ctx.enter_context(tc.psum_pool(name="psum", bufs=1))
         ctx.enter_context(tc.manual_schedule())
@@ -81,6 +83,13 @@ def tile_samplinglayer_kernel(tc, x, weight, grad_out, out):
             nc.vector.tensor_scalar_add(t_pos[:, filled : 2 * filled], t_pos[:, 0:filled], float(filled))
             filled *= 2
 
+        ones = keep.tile([P, P], F32, name="ones")
+        nc.vector.memset(ones[:], 1.0)
+        t_share = keep.tile([P, CHUNK], F32, name="t_share")
+        nc.vector.tensor_scalar_mul(t_share[:], t_pos[:, 0:CHUNK], 1.0 / P)
+        t_bank = psum.tile([P, CHUNK], F32, name="t_bank", tag="bank00")
+        nc.tensor.matmul(out=t_bank[:], lhsT=ones[:], rhs=t_share[:], start=True, stop=True)
+
         distance = keep.tile([P, K_TILES, CHUNK], F32, name="distance")
         for kt in range(K_TILES):
             nc.vector.tensor_scalar(
@@ -101,9 +110,6 @@ def tile_samplinglayer_kernel(tc, x, weight, grad_out, out):
         nc.scalar.activation(out=d_mat[:, :, 0:CHUNK], in_=d_mat[:, :, 0:CHUNK], func=ACT.Exp, scale=-0.01)
 
         banks = {}
-        for kt in range(K_TILES):
-            for h in range(HALVES):
-                banks[(kt, h)] = psum.tile([P, CHUNK], F32, name="bank%d%d" % (kt, h))
         partial = keep.tile([P, HALVES * K_TILES], F32, name="partial")
         g_codes = keep.tile([P, PASSES, K], U32, name="g_codes", align_bytes=64)
         g_scales = keep.tile([P, PASSES, K], U8, name="g_scales", align_bytes=64)
@@ -120,7 +126,9 @@ def tile_samplinglayer_kernel(tc, x, weight, grad_out, out):
             src = raw[(kind, c)][:, :, h * CHUNK : (h + 1) * CHUNK]
             if chunks[i] == ("x", 0, 1):
                 square(0, 1)
-            if i >= last - 1:
+            if i in (1, 3):
+                grouped[i] = early_pool.tile([P, CHUNK, PACK], BF16, name="early", align_bytes=64)
+            elif i >= last - 1:
                 grouped[i] = late_pool.tile([P, CHUNK, PACK], BF16, name="late%d" % (last - i), align_bytes=64)
             else:
                 grouped[i] = grouped_pool.tile([P, CHUNK, PACK], BF16, name="grouped", align_bytes=64)
@@ -130,7 +138,13 @@ def tile_samplinglayer_kernel(tc, x, weight, grad_out, out):
                 cut = 0
             else:
                 cut = CHUNK
-            if cut > 0:
+            if i == 3:
+                nc.gpsimd.tensor_scalar(
+                    out=grouped[i][:, 0:GPSIMD_COLS, :], in0=src[:, :, 0:GPSIMD_COLS].rearrange("p t c -> p c t"),
+                    scalar1=1.0, scalar2=0.0, op0=ALU.mult, op1=ALU.add,
+                )
+                interleave(nc.vector.tensor_copy, grouped[i][:, GPSIMD_COLS:CHUNK, :], src[:, :, GPSIMD_COLS:CHUNK])
+            elif cut > 0:
                 interleave(nc.vector.tensor_copy, grouped[i][:, 0:cut, :], src[:, :, 0:cut])
             if cut < CHUNK:
                 interleave(nc.scalar.copy, grouped[i][:, cut:CHUNK, :], src[:, :, cut:CHUNK])
@@ -147,6 +161,8 @@ def tile_samplinglayer_kernel(tc, x, weight, grad_out, out):
             x_scales = x_pool.tile([P, CHUNK], U8, name="x_scales", align_bytes=64)
             nc.vector.quantize_mx(out=x_codes[:].bitcast(E4M3X4), scales=x_scales[:], in_=flat)
             for kt in range(K_TILES):
+                if (kt, h) not in banks:
+                    banks[(kt, h)] = psum.tile([P, CHUNK], F32, name="bank%d%d" % (kt, h))
                 k_cols = slice(kt * P, (kt + 1) * P)
                 nc.tensor.matmul_mx(
                     out=banks[(kt, h)][:],
@@ -160,7 +176,7 @@ def tile_samplinglayer_kernel(tc, x, weight, grad_out, out):
 
         def finish_d(kt):
             nc.vector.scalar_tensor_tensor(
-                out=d_mat[:, kt, 0:CHUNK], in0=t_pos[:, 0:CHUNK], scalar=w_col[:, kt : kt + 1],
+                out=d_mat[:, kt, 0:CHUNK], in0=t_bank[:], scalar=w_col[:, kt : kt + 1],
                 in1=d_mat[:, kt, 0:CHUNK], op0=ALU.subtract, op1=ALU.mult,
             )
 
@@ -180,8 +196,9 @@ def tile_samplinglayer_kernel(tc, x, weight, grad_out, out):
             if i < last:
                 regroup(i + 1)
             quantise_and_multiply(i)
-            if PASSES // 2 <= i < PASSES // 2 + K_TILES:
-                finish_d(i - PASSES // 2)
+            if i == 1:
+                for kt in range(K_TILES):
+                    finish_d(kt)
         for kt in range(K_TILES):
             if kt > 0:
                 square(kt, 1)

@@ -22,7 +22,7 @@ CHUNK = 512
 HALVES = L // CHUNK
 K_TILES = K // P
 SHARED_COLS = 256
-GPSIMD_COLS = 384
+GPSIMD_COLS = 320
 
 FLOPS = 2 * TOKENS * L * K
 
@@ -89,6 +89,11 @@ def tile_samplinglayer_kernel(tc, x, weight, grad_out, out):
         nc.vector.tensor_scalar_mul(t_share[:], t_pos[:, 0:CHUNK], 1.0 / P)
         t_bank = psum.tile([P, CHUNK], F32, name="t_bank", tag="bank00")
         nc.tensor.matmul(out=t_bank[:], lhsT=ones[:], rhs=t_share[:], start=True, stop=True)
+
+        w_wide = keep.tile([P, K_TILES], F32, name="w_wide")
+        nc.vector.tensor_copy(out=w_wide[:], in_=w_col[:])
+        w_bank = psum.tile([P, K_TILES], F32, name="w_bank", tag="bank10")
+        nc.tensor.matmul(out=w_bank[:], lhsT=identity[:], rhs=w_wide[:], start=True, stop=True)
 
         distance = keep.tile([P, K_TILES, CHUNK], F32, name="distance")
         for kt in range(K_TILES):
@@ -176,7 +181,7 @@ def tile_samplinglayer_kernel(tc, x, weight, grad_out, out):
 
         def finish_d(kt):
             nc.vector.scalar_tensor_tensor(
-                out=d_mat[:, kt, 0:CHUNK], in0=t_bank[:], scalar=w_col[:, kt : kt + 1],
+                out=d_mat[:, kt, 0:CHUNK], in0=t_bank[:], scalar=w_bank[:, kt : kt + 1],
                 in1=d_mat[:, kt, 0:CHUNK], op0=ALU.subtract, op1=ALU.mult,
             )
 

@@ -21,8 +21,7 @@ PASSES = TOKENS // (P * PACK)
 CHUNK = 512
 HALVES = L // CHUNK
 K_TILES = K // P
-SHARED_COLS = 256
-GPSIMD_COLS = 320
+SHARED_COLS = 384
 
 FLOPS = 2 * TOKENS * L * K
 
@@ -113,6 +112,8 @@ def tile_samplinglayer_kernel(tc, x, weight, grad_out, out):
         for kt in range(K_TILES):
             square(kt, 0)
         nc.scalar.activation(out=d_mat[:, :, 0:CHUNK], in_=d_mat[:, :, 0:CHUNK], func=ACT.Exp, scale=-0.01)
+        square(0, 1)
+        nc.scalar.activation(out=d_mat[:, 0, CHUNK:L], in_=d_mat[:, 0, CHUNK:L], func=ACT.Exp, scale=-0.01)
 
         banks = {}
         partial = keep.tile([P, HALVES * K_TILES], F32, name="partial")
@@ -129,9 +130,7 @@ def tile_samplinglayer_kernel(tc, x, weight, grad_out, out):
         def regroup(i):
             kind, c, h = chunks[i]
             src = raw[(kind, c)][:, :, h * CHUNK : (h + 1) * CHUNK]
-            if chunks[i] == ("x", 0, 1):
-                square(0, 1)
-            if i in (1, 3):
+            if i == 1:
                 grouped[i] = early_pool.tile([P, CHUNK, PACK], BF16, name="early", align_bytes=64)
             elif i >= last - 1:
                 grouped[i] = late_pool.tile([P, CHUNK, PACK], BF16, name="late%d" % (last - i), align_bytes=64)
@@ -143,13 +142,7 @@ def tile_samplinglayer_kernel(tc, x, weight, grad_out, out):
                 cut = 0
             else:
                 cut = CHUNK
-            if i == 3:
-                nc.gpsimd.tensor_scalar(
-                    out=grouped[i][:, 0:GPSIMD_COLS, :], in0=src[:, :, 0:GPSIMD_COLS].rearrange("p t c -> p c t"),
-                    scalar1=1.0, scalar2=0.0, op0=ALU.mult, op1=ALU.add,
-                )
-                interleave(nc.vector.tensor_copy, grouped[i][:, GPSIMD_COLS:CHUNK, :], src[:, :, GPSIMD_COLS:CHUNK])
-            elif cut > 0:
+            if cut > 0:
                 interleave(nc.vector.tensor_copy, grouped[i][:, 0:cut, :], src[:, :, 0:cut])
             if cut < CHUNK:
                 interleave(nc.scalar.copy, grouped[i][:, cut:CHUNK, :], src[:, :, cut:CHUNK])
@@ -202,18 +195,23 @@ def tile_samplinglayer_kernel(tc, x, weight, grad_out, out):
                 regroup(i + 1)
             quantise_and_multiply(i)
             if i == 1:
+                first = early_pool.tile([P, 2, CHUNK], F32, name="early", align_bytes=64)
+                second[0] = first[:, 0, :]
+                nc.gpsimd.tensor_tensor(out=second[0], in0=distance[:, 0, :], in1=d_mat[:, 0, CHUNK:L], op=ALU.mult)
                 for kt in range(K_TILES):
                     finish_d(kt)
-        for kt in range(K_TILES):
-            if kt > 0:
-                square(kt, 1)
+        for kt in range(1, K_TILES):
+            square(kt, 1)
             nc.scalar.activation(out=d_mat[:, kt, CHUNK:L], in_=d_mat[:, kt, CHUNK:L], func=ACT.Exp, scale=-0.01)
         for pair in range(K_TILES // 2):
             late = late_pool.tile([P, 2, CHUNK], F32, name="late%d" % pair, align_bytes=64)
             for j in range(2):
-                kt = 2 * pair + j
-                second[kt] = late[:, j, :]
-                nc.gpsimd.tensor_tensor(out=second[kt], in0=distance[:, kt, :], in1=d_mat[:, kt, CHUNK:L], op=ALU.mult)
+                kt = 2 * pair + j + 1
+                if kt < K_TILES:
+                    second[kt] = late[:, j, :]
+                    nc.gpsimd.tensor_tensor(
+                        out=second[kt], in0=distance[:, kt, :], in1=d_mat[:, kt, CHUNK:L], op=ALU.mult
+                    )
         for kt in range(K_TILES):
             weigh_and_sum(kt, 0)
         for kt in range(K_TILES):

@@ -21,7 +21,8 @@ PASSES = TOKENS // (P * PACK)
 CHUNK = 512
 HALVES = L // CHUNK
 K_TILES = K // P
-SHARED_COLS = 384
+SHARED_COLS = 448
+GPSIMD_COLS = 160
 
 FLOPS = 2 * TOKENS * L * K
 
@@ -142,7 +143,13 @@ def tile_samplinglayer_kernel(tc, x, weight, grad_out, out):
                 cut = 0
             else:
                 cut = CHUNK
-            if cut > 0:
+            if i == 3:
+                nc.gpsimd.tensor_scalar(
+                    out=grouped[i][:, 0:GPSIMD_COLS, :], in0=src[:, :, 0:GPSIMD_COLS].rearrange("p t c -> p c t"),
+                    scalar1=1.0, scalar2=0.0, op0=ALU.mult, op1=ALU.add,
+                )
+                interleave(nc.vector.tensor_copy, grouped[i][:, GPSIMD_COLS:CHUNK, :], src[:, :, GPSIMD_COLS:CHUNK])
+            elif cut > 0:
                 interleave(nc.vector.tensor_copy, grouped[i][:, 0:cut, :], src[:, :, 0:cut])
             if cut < CHUNK:
                 interleave(nc.scalar.copy, grouped[i][:, cut:CHUNK, :], src[:, :, cut:CHUNK])

from contextlib import ExitStack

import concourse.mybir as mybir
from concourse.masks import make_identity

F32 = mybir.dt.float32
BF16 = mybir.dt.bfloat16
U32 = mybir.dt.uint32
U8 = mybir.dt.uint8
E4M3X4 = mybir.dt.float8_e4m3fn_x4
E5M2X4 = mybir.dt.float8_e5m2_x4
ACT = mybir.ActivationFunctionType
ALU = mybir.AluOpType

P = 128
PACK = 4
TOKENS = 4096
L = 1024
K = 512
PASSES = TOKENS // (P * PACK)
CHUNK = 512
HALVES = L // CHUNK
K_TILES = K // P
SHARED_COLS = 448
GPSIMD_COLS = 160

FLOPS = 2 * TOKENS * L * K


def tile_samplinglayer_kernel(tc, x, weight, grad_out, out):
    nc = tc.nc
    x_rows = x.rearrange("b (h j l) -> (b h) j l", h=2, j=PACK)
    g_rows = grad_out.rearrange("b (h j k) -> (b h) j k", h=2, j=PACK)

    scalar_chunks = []
    for c in range(PASSES // 2):
        scalar_chunks += [("g", c + PASSES // 2, 0), ("x", c, 1)]
    scalar_chunks += [("x", c, 1) for c in range(PASSES // 2, PASSES)]
    chunks = [("g", c, 0) for c in range(PASSES // 2)]
    for c in range(PASSES):
        chunks += [("x", c, 0), scalar_chunks[c]]
    chunks += scalar_chunks[PASSES:]
    last = len(chunks) - 1

    with ExitStack() as ctx:
        keep = ctx.enter_context(tc.tile_pool(name="keep", bufs=1))
        grouped_pool = ctx.enter_context(tc.tile_pool(name="grouped", bufs=12))
        late_pool = ctx.enter_context(tc.tile_pool(name="late", bufs=1))
        early_pool = ctx.enter_context(tc.tile_pool(name="early", bufs=1))
        x_pool = ctx.enter_context(tc.tile_pool(name="xq", bufs=6))
        product_pool = ctx.enter_context(tc.tile_pool(name="product", bufs=2))
        psum = ctx.enter_context(tc.psum_pool(name="psum", bufs=1))
        ctx.enter_context(tc.manual_schedule())

        w_col = keep.tile([P, K_TILES], BF16, name="w_col")
        with nc.allow_non_contiguous_dma(reason="512 sample positions, one to a partition"):
            nc.scalar.dma_start(out=w_col[:], in_=weight.rearrange("(a p) -> p a", p=P))
        warm = keep.tile([P, 1], F32, name="warm")
        nc.vector.memset(warm[:], 0.0)
        nc.scalar.activation(out=warm[:], in_=warm[:], func=ACT.Exp)
        loads = [("g", 0), ("g", 1), ("g", 2), ("g", 4), ("g", 3)]
        for c in range(PASSES):
            loads.append(("x", c))
            if c < PASSES // 2 - 1:
                loads.append(("g", c + PASSES // 2 + 1))
        raw = {}
        for kind, c in loads:
            rows, cols = (g_rows, K) if kind == "g" else (x_rows, L)
            raw[(kind, c)] = keep.tile([P, PACK, cols], BF16, name="raw_%s%d" % (kind, c))
            nc.sync.dma_start(out=raw[(kind, c)][:], in_=rows[c * P : (c + 1) * P])

        t_pos = keep.tile([P, L], F32, name="t_pos")
        nc.gpsimd.iota(
            t_pos[:, 0:P], pattern=[[1, P]], base=1, channel_multiplier=0,
            allow_small_or_imprecise_dtypes=True,
        )
        identity = keep.tile([P, P], F32, name="identity")
        make_identity(nc, identity[:])
        sums = keep.tile([P, P], F32, name="sums")
        nc.vector.memset(sums[:], 0.0)
        filled = P
        while filled < L:
            nc.vector.tensor_scalar_add(t_pos[:, filled : 2 * filled], t_pos[:, 0:filled], float(filled))
            filled *= 2

        ones = keep.tile([P, P], F32, name="ones")
        nc.vector.memset(ones[:], 1.0)
        t_share = keep.tile([P, CHUNK], F32, name="t_share")
        nc.vector.tensor_scalar_mul(t_share[:], t_pos[:, 0:CHUNK], 1.0 / P)
        t_bank = psum.tile([P, CHUNK], F32, name="t_bank", tag="bank00")
        nc.tensor.matmul(out=t_bank[:], lhsT=ones[:], rhs=t_share[:], start=True, stop=True)

        w_wide = keep.tile([P, K_TILES], F32, name="w_wide")
        nc.vector.tensor_copy(out=w_wide[:], in_=w_col[:])
        w_bank = psum.tile([P, K_TILES], F32, name="w_bank", tag="bank10")
        nc.tensor.matmul(out=w_bank[:], lhsT=identity[:], rhs=w_wide[:], start=True, stop=True)

        distance = keep.tile([P, K_TILES, CHUNK], F32, name="distance")
        for kt in range(K_TILES):
            nc.vector.tensor_scalar(
                out=distance[:, kt, :], in0=t_pos[:, CHUNK:L], scalar1=w_col[:, kt : kt + 1], scalar2=None,
                op0=ALU.subtract,
            )

        d_mat = keep.tile([P, K_TILES, L], F32, name="d_mat")

        def square(kt, h):
            cols = slice(h * CHUNK, (h + 1) * CHUNK)
            nc.scalar.activation(
                out=d_mat[:, kt, cols], in_=t_pos[:, cols], func=ACT.Square, bias=w_col[:, kt : kt + 1], scale=-1.0
            )

        for kt in range(K_TILES):
            square(kt, 0)
        nc.scalar.activation(out=d_mat[:, :, 0:CHUNK], in_=d_mat[:, :, 0:CHUNK], func=ACT.Exp, scale=-0.01)
        square(0, 1)
        nc.scalar.activation(out=d_mat[:, 0, CHUNK:L], in_=d_mat[:, 0, CHUNK:L], func=ACT.Exp, scale=-0.01)

        banks = {}
        partial = keep.tile([P, HALVES * K_TILES], F32, name="partial")
        g_codes = keep.tile([P, PASSES, K], U32, name="g_codes", align_bytes=64)
        g_scales = keep.tile([P, PASSES, K], U8, name="g_scales", align_bytes=64)
        grouped = {}

        def interleave(copy, dst, src):
            copy(
                out=dst.rearrange("p (c i) t -> p c t i", i=8),
                in_=src.rearrange("p t (c i) -> p c t i", i=8),
            )

        def regroup(i):
            kind, c, h = chunks[i]
            src = raw[(kind, c)][:, :, h * CHUNK : (h + 1) * CHUNK]
            if i == 1:
                grouped[i] = early_pool.tile([P, CHUNK, PACK], BF16, name="early", align_bytes=64)
            elif i >= last - 1:
                grouped[i] = late_pool.tile([P, CHUNK, PACK], BF16, name="late%d" % (last - i), align_bytes=64)
            else:
                grouped[i] = grouped_pool.tile([P, CHUNK, PACK], BF16, name="grouped", align_bytes=64)
            if i == last:
                cut = SHARED_COLS
            elif chunks[i] in scalar_chunks:
                cut = 0
            else:
                cut = CHUNK
            if i == 3:
                nc.gpsimd.tensor_scalar(
                    out=grouped[i][:, 0:GPSIMD_COLS, :], in0=src[:, :, 0:GPSIMD_COLS].rearrange("p t c -> p c t"),
                    scalar1=1.0, scalar2=0.0, op0=ALU.mult, op1=ALU.add,
                )
                interleave(nc.vector.tensor_copy, grouped[i][:, GPSIMD_COLS:CHUNK, :], src[:, :, GPSIMD_COLS:CHUNK])
            elif cut > 0:
                interleave(nc.vector.tensor_copy, grouped[i][:, 0:cut, :], src[:, :, 0:cut])
            if cut < CHUNK:
                interleave(nc.scalar.copy, grouped[i][:, cut:CHUNK, :], src[:, :, cut:CHUNK])

        def quantise_and_multiply(i):
            kind, c, h = chunks[i]
            flat = grouped[i][:].rearrange("p w t -> p (w t)")
            if kind == "g":
                nc.vector.quantize_mx(
                    out=g_codes[:, c, :].bitcast(E5M2X4), scales=g_scales[:, c, :], in_=flat
                )
                return
            x_codes = x_pool.tile([P, CHUNK], U32, name="x_codes", align_bytes=64)
            x_scales = x_pool.tile([P, CHUNK], U8, name="x_scales", align_bytes=64)
            nc.vector.quantize_mx(out=x_codes[:].bitcast(E4M3X4), scales=x_scales[:], in_=flat)
            for kt in range(K_TILES):
                if (kt, h) not in banks:
                    banks[(kt, h)] = psum.tile([P, CHUNK], F32, name="bank%d%d" % (kt, h))
                k_cols = slice(kt * P, (kt + 1) * P)
                nc.tensor.matmul_mx(
                    out=banks[(kt, h)][:],
                    lhsT=g_codes[:, c, k_cols].bitcast(E5M2X4),
                    lhsT_scale=g_scales[:, c, k_cols],
                    rhs=x_codes[:].bitcast(E4M3X4),
                    rhs_scale=x_scales[:],
                    start=(c == 0),
                    stop=(c == PASSES - 1),
                )

        def finish_d(kt):
            nc.vector.scalar_tensor_tensor(
                out=d_mat[:, kt, 0:CHUNK], in0=t_bank[:], scalar=w_bank[:, kt : kt + 1],
                in1=d_mat[:, kt, 0:CHUNK], op0=ALU.subtract, op1=ALU.mult,
            )

        second = {}

        def weigh_and_sum(kt, h):
            product = product_pool.tile([P, CHUNK], F32, name="product")
            nc.vector.scalar_tensor_tensor(
                out=product[:], in0=banks[(kt, h)][:], scalar=1.0,
                in1=d_mat[:, kt, 0:CHUNK] if h == 0 else second[kt],
                op0=ALU.mult, op1=ALU.mult,
                accum_out=partial[:, h * K_TILES + kt : h * K_TILES + kt + 1],
            )

        regroup(0)
        for i in range(len(chunks)):
            if i < last:
                regroup(i + 1)
            quantise_and_multiply(i)
            if i == 1:
                first = early_pool.tile([P, 2, CHUNK], F32, name="early", align_bytes=64)
                second[0] = first[:, 0, :]
                nc.gpsimd.tensor_tensor(out=second[0], in0=distance[:, 0, :], in1=d_mat[:, 0, CHUNK:L], op=ALU.mult)
                for kt in range(K_TILES):
                    finish_d(kt)
        for kt in range(1, K_TILES):
            square(kt, 1)
            nc.scalar.activation(out=d_mat[:, kt, CHUNK:L], in_=d_mat[:, kt, CHUNK:L], func=ACT.Exp, scale=-0.01)
        for pair in range(K_TILES // 2):
            late = late_pool.tile([P, 2, CHUNK], F32, name="late%d" % pair, align_bytes=64)
            for j in range(2):
                kt = 2 * pair + j + 1
                if kt < K_TILES:
                    second[kt] = late[:, j, :]
                    nc.gpsimd.tensor_tensor(
                        out=second[kt], in0=distance[:, kt, :], in1=d_mat[:, kt, CHUNK:L], op=ALU.mult
                    )
        for kt in range(K_TILES):
            weigh_and_sum(kt, 0)
        for kt in range(K_TILES):
            weigh_and_sum(kt, 1)

        nc.vector.tensor_tensor(
            out=sums[:, 0:K_TILES], in0=partial[:, 0:K_TILES], in1=partial[:, K_TILES : 2 * K_TILES], op=ALU.add
        )
        flipped = psum.tile([P, P], F32, name="flipped", tag="bank00")
        nc.tensor.transpose(flipped[:], sums[:], identity[:])
        out_rows = keep.tile([P, P], F32, name="out_rows")
        nc.scalar.activation(out=out_rows[:], in_=flipped[:], func=ACT.Copy, scale=0.02)
        nc.sync.dma_start(out=out.rearrange("(a k) -> a k", a=K_TILES), in_=out_rows[0:K_TILES, :])
